import numpy as np
import ml_dtypes

BF16 = ml_dtypes.bfloat16


def bf(x):
    return np.asarray(x, np.float32).astype(BF16)


def f32(x):
    return np.asarray(x, np.float32)


def f64(x):
    return np.asarray(x).astype(np.float64)


def striped(idx):
    return np.tile(idx.reshape(-1, 16).T, (8, 1))


F, S, DEG, A, M, N, H, K = 128, 512, 4, 4, 512, 2048, 256, 8


def sigmoid(v):
    return 1.0 / (1.0 + np.exp(-v))


def setup_inputs():
    lim = 1.0 / np.sqrt(F)
    return {"x": bf(np.random.standard_normal((F, S))), "w_cen": bf(np.random.uniform(-lim, lim, (F, M))), "w_nbr": bf(np.random.uniform(-lim, lim, (F, M))), "offs": striped(np.concatenate([np.random.permutation(S)[:H] for _ in range(K)]))}


def reference(x, w_cen, w_nbr, offs):
    idx = offs[:16].T.reshape(-1)
    nbr = f64(x)[:, idx]
    cen = f64(w_cen).T @ f64(x)
    z = (f64(w_nbr).T @ nbr).reshape(M, DEG, S) + cen[:, None, :]
    mask = sigmoid(z).reshape(A, F, N)
    return (mask * nbr[None, :, :]).reshape(M, N)

@@ -1,0 +1,71 @@
+import concourse.mybir as mybir
+from concourse.masks import make_identity
+
+BF16, F32, U16 = mybir.dt.bfloat16, mybir.dt.float32, mybir.dt.uint16
+
+P = 128
+NODES = 512
+DEGREE = 4
+MASKS = 4
+LIST = DEGREE * NODES
+RUN_COLS = NODES // 16
+PIECE = 64
+
+FLOPS = 2 * P * (MASKS * P) * (LIST + NODES)
+
+
+def tile_mma_kernel(tc, x, w_cen, w_nbr, offs, out):
+    nc = tc.nc
+    sigmoid = mybir.ActivationFunctionType.Sigmoid
+    with (
+        tc.tile_pool(name="held", bufs=1) as held,
+        tc.tile_pool(name="work", bufs=6) as work,
+        tc.psum_pool(name="banks", bufs=8) as banks,
+    ):
+        offsets = held.tile([P, LIST // 16], U16, name="offsets")
+        nc.sync.dma_start(offsets[:], offs)
+        nodes = held.tile([P, NODES], BF16, name="nodes")
+        nc.scalar.dma_start(nodes[:], x)
+        cen_weights = held.tile([P, MASKS * P], BF16, name="cen_weights")
+        nc.scalar.dma_start(cen_weights[:], w_cen)
+        identity = held.tile([P, P], BF16, name="identity")
+        make_identity(nc, identity[:])
+        nbr_weights = held.tile([P, MASKS * P], BF16, name="nbr_weights")
+        nc.gpsimd.dma_start(nbr_weights[:], w_nbr)
+        scratch = held.tile([P, 1], F32, name="scratch")
+        nc.vector.memset(scratch[:], 0.0)
+        scratch_out = held.tile([P, 1], F32, name="scratch_out")
+        nc.scalar.activation(scratch_out[:], scratch[:], sigmoid)
+
+        runs = [offsets[:, d * RUN_COLS : (d + 1) * RUN_COLS] for d in range(DEGREE)]
+
+        neighbours = []
+        for d in range(DEGREE):
+            gathered = banks.tile([P, NODES], F32, name="bank")
+            nc.tensor.matmul(gathered[:], identity[:], nodes[:].indirect(runs[d]), start=True, stop=True)
+            kept = held.tile([P, NODES], F32, name=f"neighbours{d}")
+            nc.vector.tensor_copy(kept[:], gathered[:])
+            neighbours.append(kept)
+
+        for d in range(DEGREE):
+            z_of_mask = []
+            for a in range(MASKS):
+                z = banks.tile([P, NODES], F32, name="bank")
+                nc.tensor.matmul(
+                    z[:], nbr_weights[:, a * P : (a + 1) * P], nodes[:].indirect(runs[d]), start=True, stop=False
+                )
+                z_of_mask.append(z)
+            for a in range(MASKS):
+                block = slice(a * P, (a + 1) * P)
+                z = z_of_mask[a]
+                for first in range(0, NODES, PIECE):
+                    piece = slice(first, first + PIECE)
+                    nc.tensor.matmul(
+                        z[:, piece], cen_weights[:, block], nodes[:, piece],
+                        start=False, stop=(first + PIECE == NODES),
+                    )
+                mask = work.tile([P, NODES], F32, name="mask")
+                nc.scalar.activation(mask[:], z[:], sigmoid)
+                masked = work.tile([P, NODES], F32, name="masked")
+                nc.vector.tensor_tensor(masked[:], mask[:], neighbours[d][:], mybir.AluOpType.mult)
+                nc.sync.dma_start(out[block, d * NODES : (d + 1) * NODES], masked[:])

@@ -10,6 +10,7 @@ MASKS = 4
 LIST = DEGREE * NODES
 RUN_COLS = NODES // 16
 PIECE = 64
+WARM_UP = 4
 
 FLOPS = 2 * P * (MASKS * P) * (LIST + NODES)
 
@@ -36,6 +37,12 @@ def tile_mma_kernel(tc, x, w_cen, w_nbr, offs, out):
         nc.vector.memset(scratch[:], 0.0)
         scratch_out = held.tile([P, 1], F32, name="scratch_out")
         nc.scalar.activation(scratch_out[:], scratch[:], sigmoid)
+
+        zeros = held.tile([P, NODES], BF16, name="zeros")
+        nc.vector.memset(zeros[:], 0.0)
+        unused = banks.tile([P, NODES], F32, name="bank")
+        for repeat in range(WARM_UP):
+            nc.tensor.matmul(unused[:], zeros[:, 0:P], zeros[:], start=True, stop=True)
 
         runs = [offsets[:, d * RUN_COLS : (d + 1) * RUN_COLS] for d in range(DEGREE)]
 

@@ -10,7 +10,6 @@ MASKS = 4
 LIST = DEGREE * NODES
 RUN_COLS = NODES // 16
 PIECE = 64
-WARM_UP = 4
 
 FLOPS = 2 * P * (MASKS * P) * (LIST + NODES)
 
@@ -29,20 +28,14 @@ def tile_mma_kernel(tc, x, w_cen, w_nbr, offs, out):
         nc.scalar.dma_start(nodes[:], x)
         cen_weights = held.tile([P, MASKS * P], BF16, name="cen_weights")
         nc.scalar.dma_start(cen_weights[:], w_cen)
+        nbr_weights = held.tile([P, MASKS * P], BF16, name="nbr_weights")
+        nc.sync.dma_start(nbr_weights[:], w_nbr)
         identity = held.tile([P, P], BF16, name="identity")
         make_identity(nc, identity[:])
-        nbr_weights = held.tile([P, MASKS * P], BF16, name="nbr_weights")
-        nc.gpsimd.dma_start(nbr_weights[:], w_nbr)
         scratch = held.tile([P, 1], F32, name="scratch")
         nc.vector.memset(scratch[:], 0.0)
         scratch_out = held.tile([P, 1], F32, name="scratch_out")
         nc.scalar.activation(scratch_out[:], scratch[:], sigmoid)
-
-        zeros = held.tile([P, NODES], BF16, name="zeros")
-        nc.vector.memset(zeros[:], 0.0)
-        unused = banks.tile([P, NODES], F32, name="bank")
-        for repeat in range(WARM_UP):
-            nc.tensor.matmul(unused[:], zeros[:, 0:P], zeros[:], start=True, stop=True)
 
         runs = [offsets[:, d * RUN_COLS : (d + 1) * RUN_COLS] for d in range(DEGREE)]
 

@@ -10,6 +10,7 @@ MASKS = 4
 LIST = DEGREE * NODES
 RUN_COLS = NODES // 16
 PIECE = 64
+HALF = NODES // 2
 
 FLOPS = 2 * P * (MASKS * P) * (LIST + NODES)
 
@@ -37,35 +38,55 @@ def tile_mma_kernel(tc, x, w_cen, w_nbr, offs, out):
         scratch_out = held.tile([P, 1], F32, name="scratch_out")
         nc.scalar.activation(scratch_out[:], scratch[:], sigmoid)
 
-        runs = [offsets[:, d * RUN_COLS : (d + 1) * RUN_COLS] for d in range(DEGREE)]
+        def centre_part(z, a, opens):
+            for first in range(0, NODES, PIECE):
+                piece = slice(first, first + PIECE)
+                nc.tensor.matmul(
+                    z[:, piece], cen_weights[:, a * P : (a + 1) * P], nodes[:, piece],
+                    start=(opens and first == 0), stop=(not opens and first + PIECE == NODES),
+                )
+
+        def finish(z, d, a):
+            mask = work.tile([P, NODES], F32, name="mask")
+            nc.scalar.activation(mask[:], z[:], sigmoid)
+            masked = work.tile([P, NODES], F32, name="masked")
+            nc.vector.tensor_tensor(masked[:], mask[:], neighbours[d][:], mybir.AluOpType.mult)
+            nc.sync.dma_start(out[a * P : (a + 1) * P, d * NODES : (d + 1) * NODES], masked[:])
 
         neighbours = []
         for d in range(DEGREE):
             gathered = banks.tile([P, NODES], F32, name="bank")
-            nc.tensor.matmul(gathered[:], identity[:], nodes[:].indirect(runs[d]), start=True, stop=True)
+            run = offsets[:, d * RUN_COLS : (d + 1) * RUN_COLS]
+            nc.tensor.matmul(gathered[:], identity[:], nodes[:].indirect(run), start=True, stop=True)
             kept = held.tile([P, NODES], F32, name=f"neighbours{d}")
             nc.vector.tensor_copy(kept[:], gathered[:])
             neighbours.append(kept)
 
-        for d in range(DEGREE):
+        for d in range(DEGREE - 1):
+            run = offsets[:, d * RUN_COLS : (d + 1) * RUN_COLS]
             z_of_mask = []
             for a in range(MASKS):
                 z = banks.tile([P, NODES], F32, name="bank")
                 nc.tensor.matmul(
-                    z[:], nbr_weights[:, a * P : (a + 1) * P], nodes[:].indirect(runs[d]), start=True, stop=False
+                    z[:], nbr_weights[:, a * P : (a + 1) * P], nodes[:].indirect(run), start=True, stop=False
                 )
                 z_of_mask.append(z)
             for a in range(MASKS):
-                block = slice(a * P, (a + 1) * P)
-                z = z_of_mask[a]
-                for first in range(0, NODES, PIECE):
-                    piece = slice(first, first + PIECE)
-                    nc.tensor.matmul(
-                        z[:, piece], cen_weights[:, block], nodes[:, piece],
-                        start=False, stop=(first + PIECE == NODES),
-                    )
-                mask = work.tile([P, NODES], F32, name="mask")
-                nc.scalar.activation(mask[:], z[:], sigmoid)
-                masked = work.tile([P, NODES], F32, name="masked")
-                nc.vector.tensor_tensor(masked[:], mask[:], neighbours[d][:], mybir.AluOpType.mult)
-                nc.sync.dma_start(out[block, d * NODES : (d + 1) * NODES], masked[:])
+                centre_part(z_of_mask[a], a, opens=False)
+                finish(z_of_mask[a], d, a)
+
+        d = DEGREE - 1
+        z_of_mask = []
+        for a in range(MASKS):
+            z = banks.tile([P, NODES], F32, name="bank")
+            centre_part(z, a, opens=True)
+            z_of_mask.append(z)
+        for a in range(MASKS):
+            z = z_of_mask[a]
+            for first in range(0, NODES, HALF):
+                entries = offsets[:, (d * NODES + first) // 16 : (d * NODES + first + HALF) // 16]
+                nc.tensor.matmul(
+                    z[:, first : first + HALF], nbr_weights[:, a * P : (a + 1) * P], nodes[:].indirect(entries),
+                    start=False, stop=(first + HALF == NODES),
+                )
+            finish(z, d, a)

@@ -9,7 +9,7 @@ DEGREE = 4
 MASKS = 4
 LIST = DEGREE * NODES
 RUN_COLS = NODES // 16
-PIECE = 64
+PIECE = 128
 HALF = NODES // 2
 
 FLOPS = 2 * P * (MASKS * P) * (LIST + NODES)
@@ -62,31 +62,24 @@ def tile_mma_kernel(tc, x, w_cen, w_nbr, offs, out):
             nc.vector.tensor_copy(kept[:], gathered[:])
             neighbours.append(kept)
 
-        for d in range(DEGREE - 1):
-            run = offsets[:, d * RUN_COLS : (d + 1) * RUN_COLS]
-            z_of_mask = []
+        def neighbour_part(z, d, a, first, entries, opens):
+            listed = offsets[:, (d * NODES + first) // 16 : (d * NODES + first + entries) // 16]
+            nc.tensor.matmul(
+                z[:, first : first + entries], nbr_weights[:, a * P : (a + 1) * P], nodes[:].indirect(listed),
+                start=opens, stop=(not opens and first + entries == NODES),
+            )
+
+        for d in range(0, DEGREE, 2):
+            z_of_mask = [banks.tile([P, NODES], F32, name="bank") for a in range(MASKS)]
             for a in range(MASKS):
-                z = banks.tile([P, NODES], F32, name="bank")
-                nc.tensor.matmul(
-                    z[:], nbr_weights[:, a * P : (a + 1) * P], nodes[:].indirect(run), start=True, stop=False
-                )
-                z_of_mask.append(z)
+                neighbour_part(z_of_mask[a], d, a, 0, NODES, opens=True)
             for a in range(MASKS):
                 centre_part(z_of_mask[a], a, opens=False)
                 finish(z_of_mask[a], d, a)
-
-        d = DEGREE - 1
-        z_of_mask = []
-        for a in range(MASKS):
-            z = banks.tile([P, NODES], F32, name="bank")
-            centre_part(z, a, opens=True)
-            z_of_mask.append(z)
-        for a in range(MASKS):
-            z = z_of_mask[a]
-            for first in range(0, NODES, HALF):
-                entries = offsets[:, (d * NODES + first) // 16 : (d * NODES + first + HALF) // 16]
-                nc.tensor.matmul(
-                    z[:, first : first + HALF], nbr_weights[:, a * P : (a + 1) * P], nodes[:].indirect(entries),
-                    start=False, stop=(first + HALF == NODES),
-                )
-            finish(z, d, a)
+            z_of_mask = [banks.tile([P, NODES], F32, name="bank") for a in range(MASKS)]
+            for a in range(MASKS):
+                centre_part(z_of_mask[a], a, opens=True)
+            for a in range(MASKS):
+                for first in range(0, NODES, HALF):
+                    neighbour_part(z_of_mask[a], d + 1, a, first, HALF, opens=False)
+                finish(z_of_mask[a], d + 1, a)

@@ -33,10 +33,6 @@ def tile_mma_kernel(tc, x, w_cen, w_nbr, offs, out):
         nc.sync.dma_start(nbr_weights[:], w_nbr)
         identity = held.tile([P, P], BF16, name="identity")
         make_identity(nc, identity[:])
-        scratch = held.tile([P, 1], F32, name="scratch")
-        nc.vector.memset(scratch[:], 0.0)
-        scratch_out = held.tile([P, 1], F32, name="scratch_out")
-        nc.scalar.activation(scratch_out[:], scratch[:], sigmoid)
 
         def centre_part(z, a, opens):
             for first in range(0, NODES, PIECE):

@@ -11,6 +11,7 @@ LIST = DEGREE * NODES
 RUN_COLS = NODES // 16
 PIECE = 128
 HALF = NODES // 2
+TENSOR_MASKS = MASKS - 1
 
 FLOPS = 2 * P * (MASKS * P) * (LIST + NODES)
 
@@ -23,31 +24,76 @@ def tile_mma_kernel(tc, x, w_cen, w_nbr, offs, out):
         tc.tile_pool(name="work", bufs=6) as work,
         tc.psum_pool(name="banks", bufs=8) as banks,
     ):
-        offsets = held.tile([P, LIST // 16], U16, name="offsets")
-        nc.sync.dma_start(offsets[:], offs)
         nodes = held.tile([P, NODES], BF16, name="nodes")
         nc.scalar.dma_start(nodes[:], x)
         cen_weights = held.tile([P, MASKS * P], BF16, name="cen_weights")
-        nc.scalar.dma_start(cen_weights[:], w_cen)
+        nc.sync.dma_start(cen_weights[:], w_cen)
+        offsets = held.tile([P, LIST // 16], U16, name="offsets")
+        nc.sync.dma_start(offsets[:], offs)
         nbr_weights = held.tile([P, MASKS * P], BF16, name="nbr_weights")
         nc.sync.dma_start(nbr_weights[:], w_nbr)
         identity = held.tile([P, P], BF16, name="identity")
         make_identity(nc, identity[:])
 
-        def centre_part(z, a, opens):
+        add, mult = mybir.AluOpType.add, mybir.AluOpType.mult
+
+        def centre_part(z, a, opens, closes):
             for first in range(0, NODES, PIECE):
                 piece = slice(first, first + PIECE)
                 nc.tensor.matmul(
                     z[:, piece], cen_weights[:, a * P : (a + 1) * P], nodes[:, piece],
-                    start=(opens and first == 0), stop=(not opens and first + PIECE == NODES),
+                    start=(opens and first == 0), stop=(closes and first + PIECE == NODES),
                 )
+
+        def neighbour_part(z, d, a, first, entries, opens, closes):
+            listed = offsets[:, (d * NODES + first) // 16 : (d * NODES + first + entries) // 16]
+            nc.tensor.matmul(
+                z[:, first : first + entries], nbr_weights[:, a * P : (a + 1) * P], nodes[:].indirect(listed),
+                start=opens, stop=(closes and first + entries == NODES),
+            )
 
         def finish(z, d, a):
             mask = work.tile([P, NODES], F32, name="mask")
             nc.scalar.activation(mask[:], z[:], sigmoid)
             masked = work.tile([P, NODES], F32, name="masked")
-            nc.vector.tensor_tensor(masked[:], mask[:], neighbours[d][:], mybir.AluOpType.mult)
+            nc.vector.tensor_tensor(masked[:], mask[:], neighbours[d][:], mult)
             nc.sync.dma_start(out[a * P : (a + 1) * P, d * NODES : (d + 1) * NODES], masked[:])
+
+        def open_by_gather(d):
+            sums = [banks.tile([P, NODES], F32, name="bank") for a in range(TENSOR_MASKS)]
+            for a in range(TENSOR_MASKS):
+                neighbour_part(sums[a], d, a, 0, NODES, opens=True, closes=False)
+            return sums
+
+        def close_by_centre(sums, d):
+            for a in range(TENSOR_MASKS):
+                centre_part(sums[a], a, opens=False, closes=True)
+                finish(sums[a], d, a)
+
+        def open_by_centre():
+            sums = [banks.tile([P, NODES], F32, name="bank") for a in range(TENSOR_MASKS)]
+            for a in range(TENSOR_MASKS):
+                centre_part(sums[a], a, opens=True, closes=False)
+            return sums
+
+        def close_by_gather(sums, d):
+            for a in range(TENSOR_MASKS):
+                for first in range(0, NODES, HALF):
+                    neighbour_part(sums[a], d, a, first, HALF, opens=False, closes=True)
+                finish(sums[a], d, a)
+
+        centre_bank = banks.tile([P, NODES], F32, name="bank")
+        nc.tensor.matmul(centre_bank[:], cen_weights[:, TENSOR_MASKS * P :], nodes[:], start=True, stop=True)
+        centre_kept = held.tile([P, NODES], F32, name="centre_kept")
+        nc.vector.tensor_copy(centre_kept[:], centre_bank[:])
+
+        last_mask_sums = []
+        for d in range(DEGREE):
+            product = banks.tile([P, NODES], F32, name="bank")
+            neighbour_part(product, d, MASKS - 1, 0, NODES, opens=True, closes=True)
+            z = held.tile([P, NODES], F32, name=f"z{d}")
+            nc.vector.tensor_tensor(z[:], product[:], centre_kept[:], add)
+            last_mask_sums.append(z)
 
         neighbours = []
         for d in range(DEGREE):
@@ -58,24 +104,11 @@ def tile_mma_kernel(tc, x, w_cen, w_nbr, offs, out):
             nc.vector.tensor_copy(kept[:], gathered[:])
             neighbours.append(kept)
 
-        def neighbour_part(z, d, a, first, entries, opens):
-            listed = offsets[:, (d * NODES + first) // 16 : (d * NODES + first + entries) // 16]
-            nc.tensor.matmul(
-                z[:, first : first + entries], nbr_weights[:, a * P : (a + 1) * P], nodes[:].indirect(listed),
-                start=opens, stop=(not opens and first + entries == NODES),
-            )
+        for d in range(DEGREE):
+            finish(last_mask_sums[d], d, MASKS - 1)
 
         for d in range(0, DEGREE, 2):
-            z_of_mask = [banks.tile([P, NODES], F32, name="bank") for a in range(MASKS)]
-            for a in range(MASKS):
-                neighbour_part(z_of_mask[a], d, a, 0, NODES, opens=True)
-            for a in range(MASKS):
-                centre_part(z_of_mask[a], a, opens=False)
-                finish(z_of_mask[a], d, a)
-            z_of_mask = [banks.tile([P, NODES], F32, name="bank") for a in range(MASKS)]
-            for a in range(MASKS):
-                centre_part(z_of_mask[a], a, opens=True)
-            for a in range(MASKS):
-                for first in range(0, NODES, HALF):
-                    neighbour_part(z_of_mask[a], d + 1, a, first, HALF, opens=False)
-                finish(z_of_mask[a], d + 1, a)
+            sums = open_by_gather(d)
+            close_by_centre(sums, d)
+            sums = open_by_centre()
+            close_by_gather(sums, d + 1)

@@ -101,7 +101,7 @@ def tile_mma_kernel(tc, x, w_cen, w_nbr, offs, out):
             run = offsets[:, d * RUN_COLS : (d + 1) * RUN_COLS]
             nc.tensor.matmul(gathered[:], identity[:], nodes[:].indirect(run), start=True, stop=True)
             kept = held.tile([P, NODES], F32, name=f"neighbours{d}")
-            nc.vector.tensor_copy(kept[:], gathered[:])
+            nc.scalar.copy(kept[:], gathered[:])
             neighbours.append(kept)
 
         for d in range(DEGREE):

@@ -31,7 +31,7 @@ def tile_mma_kernel(tc, x, w_cen, w_nbr, offs, out):
         offsets = held.tile([P, LIST // 16], U16, name="offsets")
         nc.sync.dma_start(offsets[:], offs)
         nbr_weights = held.tile([P, MASKS * P], BF16, name="nbr_weights")
-        nc.sync.dma_start(nbr_weights[:], w_nbr)
+        nc.scalar.dma_start(nbr_weights[:], w_nbr)
         identity = held.tile([P, P], BF16, name="identity")
         make_identity(nc, identity[:])
 

@@ -24,14 +24,19 @@ def tile_mma_kernel(tc, x, w_cen, w_nbr, offs, out):
         tc.tile_pool(name="work", bufs=6) as work,
         tc.psum_pool(name="banks", bufs=8) as banks,
     ):
+        others = TENSOR_MASKS * P
         nodes = held.tile([P, NODES], BF16, name="nodes")
         nc.scalar.dma_start(nodes[:], x)
-        cen_weights = held.tile([P, MASKS * P], BF16, name="cen_weights")
-        nc.sync.dma_start(cen_weights[:], w_cen)
+        last_cen_weights = held.tile([P, P], BF16, name="last_cen_weights")
+        nc.sync.dma_start(last_cen_weights[:], w_cen[:, others:])
         offsets = held.tile([P, LIST // 16], U16, name="offsets")
         nc.sync.dma_start(offsets[:], offs)
-        nbr_weights = held.tile([P, MASKS * P], BF16, name="nbr_weights")
-        nc.scalar.dma_start(nbr_weights[:], w_nbr)
+        last_nbr_weights = held.tile([P, P], BF16, name="last_nbr_weights")
+        nc.sync.dma_start(last_nbr_weights[:], w_nbr[:, others:])
+        nbr_weights = held.tile([P, others], BF16, name="nbr_weights")
+        nc.scalar.dma_start(nbr_weights[:], w_nbr[:, :others])
+        cen_weights = held.tile([P, others], BF16, name="cen_weights")
+        nc.sync.dma_start(cen_weights[:], w_cen[:, :others])
         identity = held.tile([P, P], BF16, name="identity")
         make_identity(nc, identity[:])
 
@@ -45,12 +50,15 @@ def tile_mma_kernel(tc, x, w_cen, w_nbr, offs, out):
                     start=(opens and first == 0), stop=(closes and first + PIECE == NODES),
                 )
 
-        def neighbour_part(z, d, a, first, entries, opens, closes):
+        def neighbour_part(z, d, weights, first, entries, opens, closes):
             listed = offsets[:, (d * NODES + first) // 16 : (d * NODES + first + entries) // 16]
             nc.tensor.matmul(
-                z[:, first : first + entries], nbr_weights[:, a * P : (a + 1) * P], nodes[:].indirect(listed),
+                z[:, first : first + entries], weights, nodes[:].indirect(listed),
                 start=opens, stop=(closes and first + entries == NODES),
             )
+
+        def nbr_block(a):
+            return nbr_weights[:, a * P : (a + 1) * P]
 
         def finish(z, d, a):
             mask = work.tile([P, NODES], F32, name="mask")
@@ -62,7 +70,7 @@ def tile_mma_kernel(tc, x, w_cen, w_nbr, offs, out):
         def open_by_gather(d):
             sums = [banks.tile([P, NODES], F32, name="bank") for a in range(TENSOR_MASKS)]
             for a in range(TENSOR_MASKS):
-                neighbour_part(sums[a], d, a, 0, NODES, opens=True, closes=False)
+                neighbour_part(sums[a], d, nbr_block(a), 0, NODES, opens=True, closes=False)
             return sums
 
         def close_by_centre(sums, d):
@@ -79,18 +87,18 @@ def tile_mma_kernel(tc, x, w_cen, w_nbr, offs, out):
         def close_by_gather(sums, d):
             for a in range(TENSOR_MASKS):
                 for first in range(0, NODES, HALF):
-                    neighbour_part(sums[a], d, a, first, HALF, opens=False, closes=True)
+                    neighbour_part(sums[a], d, nbr_block(a), first, HALF, opens=False, closes=True)
                 finish(sums[a], d, a)
 
         centre_bank = banks.tile([P, NODES], F32, name="bank")
-        nc.tensor.matmul(centre_bank[:], cen_weights[:, TENSOR_MASKS * P :], nodes[:], start=True, stop=True)
+        nc.tensor.matmul(centre_bank[:], last_cen_weights[:], nodes[:], start=True, stop=True)
         centre_kept = held.tile([P, NODES], F32, name="centre_kept")
         nc.vector.tensor_copy(centre_kept[:], centre_bank[:])
 
         last_mask_sums = []
         for d in range(DEGREE):
             product = banks.tile([P, NODES], F32, name="bank")
-            neighbour_part(product, d, MASKS - 1, 0, NODES, opens=True, closes=True)
+            neighbour_part(product, d, last_nbr_weights[:], 0, NODES, opens=True, closes=True)
             z = held.tile([P, NODES], F32, name=f"z{d}")
             nc.vector.tensor_tensor(z[:], product[:], centre_kept[:], add)
             last_mask_sums.append(z)

@@ -9,7 +9,8 @@ DEGREE = 4
 MASKS = 4
 LIST = DEGREE * NODES
 RUN_COLS = NODES // 16
-PIECE = 128
+APART = 24
+STEP = 16
 HALF = NODES // 2
 TENSOR_MASKS = MASKS - 1
 
@@ -42,12 +43,12 @@ def tile_mma_kernel(tc, x, w_cen, w_nbr, offs, out):
 
         add, mult = mybir.AluOpType.add, mybir.AluOpType.mult
 
-        def centre_part(z, a, opens, closes):
-            for first in range(0, NODES, PIECE):
-                piece = slice(first, first + PIECE)
+        def centre_part(z, a, pieces, opens, closes):
+            edges = [NODES * i // (pieces * STEP) * STEP for i in range(pieces + 1)]
+            for first, end in zip(edges[:-1], edges[1:]):
                 nc.tensor.matmul(
-                    z[:, piece], cen_weights[:, a * P : (a + 1) * P], nodes[:, piece],
-                    start=(opens and first == 0), stop=(closes and first + PIECE == NODES),
+                    z[:, first:end], cen_weights[:, a * P : (a + 1) * P], nodes[:, first:end],
+                    start=(opens and first == 0), stop=(closes and end == NODES),
                 )
 
         def neighbour_part(z, d, weights, first, entries, opens, closes):
@@ -60,35 +61,38 @@ def tile_mma_kernel(tc, x, w_cen, w_nbr, offs, out):
         def nbr_block(a):
             return nbr_weights[:, a * P : (a + 1) * P]
 
-        def finish(z, d, a):
+        def finish(z, d, a, parts=1):
             mask = work.tile([P, NODES], F32, name="mask")
-            nc.scalar.activation(mask[:], z[:], sigmoid)
             masked = work.tile([P, NODES], F32, name="masked")
-            nc.vector.tensor_tensor(masked[:], mask[:], neighbours[d][:], mult)
-            nc.sync.dma_start(out[a * P : (a + 1) * P, d * NODES : (d + 1) * NODES], masked[:])
+            for part in range(parts):
+                cols = slice(part * NODES // parts, (part + 1) * NODES // parts)
+                nc.scalar.activation(mask[:, cols], z[:, cols], sigmoid)
+                nc.vector.tensor_tensor(masked[:, cols], mask[:, cols], neighbours[d][:, cols], mult)
+                stored = slice(d * NODES + cols.start, d * NODES + cols.stop)
+                nc.sync.dma_start(out[a * P : (a + 1) * P, stored], masked[:, cols])
 
-        def open_by_gather(d):
-            sums = [banks.tile([P, NODES], F32, name="bank") for a in range(TENSOR_MASKS)]
-            for a in range(TENSOR_MASKS):
-                neighbour_part(sums[a], d, nbr_block(a), 0, NODES, opens=True, closes=False)
+        def open_by_gather(units):
+            sums = [banks.tile([P, NODES], F32, name="bank") for unit in units]
+            for z, (d, a) in zip(sums, units):
+                neighbour_part(z, d, nbr_block(a), 0, NODES, opens=True, closes=False)
             return sums
 
-        def close_by_centre(sums, d):
-            for a in range(TENSOR_MASKS):
-                centre_part(sums[a], a, opens=False, closes=True)
-                finish(sums[a], d, a)
+        def close_by_centre(sums, units, pieces, parts=1):
+            for z, (d, a) in zip(sums, units):
+                centre_part(z, a, pieces, opens=False, closes=True)
+                finish(z, d, a, parts)
 
-        def open_by_centre():
-            sums = [banks.tile([P, NODES], F32, name="bank") for a in range(TENSOR_MASKS)]
-            for a in range(TENSOR_MASKS):
-                centre_part(sums[a], a, opens=True, closes=False)
+        def open_by_centre(units, pieces):
+            sums = [banks.tile([P, NODES], F32, name="bank") for unit in units]
+            for z, (d, a) in zip(sums, units):
+                centre_part(z, a, pieces, opens=True, closes=False)
             return sums
 
-        def close_by_gather(sums, d):
-            for a in range(TENSOR_MASKS):
+        def close_by_gather(sums, units):
+            for z, (d, a) in zip(sums, units):
                 for first in range(0, NODES, HALF):
-                    neighbour_part(sums[a], d, nbr_block(a), first, HALF, opens=False, closes=True)
-                finish(sums[a], d, a)
+                    neighbour_part(z, d, nbr_block(a), first, HALF, opens=False, closes=True)
+                finish(z, d, a)
 
         centre_bank = banks.tile([P, NODES], F32, name="bank")
         nc.tensor.matmul(centre_bank[:], last_cen_weights[:], nodes[:], start=True, stop=True)
@@ -115,8 +119,19 @@ def tile_mma_kernel(tc, x, w_cen, w_nbr, offs, out):
         for d in range(DEGREE):
             finish(last_mask_sums[d], d, MASKS - 1)
 
-        for d in range(0, DEGREE, 2):
-            sums = open_by_gather(d)
-            close_by_centre(sums, d)
-            sums = open_by_centre()
-            close_by_gather(sums, d + 1)
+        units = [(d, a) for d in range(DEGREE) for a in range(TENSOR_MASKS)]
+        gap_sums = (8, 3)
+        first = 0
+        for count in gap_sums:
+            here = units[first : first + count]
+            first += count
+            pieces = -(-APART // count)
+            before = here[: (count + 1) // 2]
+            behind = here[(count + 1) // 2 :]
+            sums = open_by_gather(before)
+            close_by_centre(sums, before, pieces)
+            sums = open_by_centre(behind, pieces)
+            close_by_gather(sums, behind)
+        tail = units[first:]
+        sums = open_by_gather(tail)
+        close_by_centre(sums, tail, pieces=2, parts=2)

@@ -27,7 +27,8 @@ def tile_mma_kernel(tc, x, w_cen, w_nbr, offs, out):
     ):
         others = TENSOR_MASKS * P
         nodes = held.tile([P, NODES], BF16, name="nodes")
-        nc.scalar.dma_start(nodes[:], x)
+        for first in range(0, NODES, HALF):
+            nc.scalar.dma_start(nodes[:, first : first + HALF], x[:, first : first + HALF])
         last_cen_weights = held.tile([P, P], BF16, name="last_cen_weights")
         nc.sync.dma_start(last_cen_weights[:], w_cen[:, others:])
         offsets = held.tile([P, LIST // 16], U16, name="offsets")
@@ -95,7 +96,12 @@ def tile_mma_kernel(tc, x, w_cen, w_nbr, offs, out):
                 finish(z, d, a)
 
         centre_bank = banks.tile([P, NODES], F32, name="bank")
-        nc.tensor.matmul(centre_bank[:], last_cen_weights[:], nodes[:], start=True, stop=True)
+        for first in range(0, NODES, HALF):
+            cols = slice(first, first + HALF)
+            nc.tensor.matmul(
+                centre_bank[:, cols], last_cen_weights[:], nodes[:, cols],
+                start=(first == 0), stop=(first + HALF == NODES),
+            )
         centre_kept = held.tile([P, NODES], F32, name="centre_kept")
         nc.vector.tensor_copy(centre_kept[:], centre_bank[:])
 

@@ -36,7 +36,7 @@ def tile_mma_kernel(tc, x, w_cen, w_nbr, offs, out):
         last_nbr_weights = held.tile([P, P], BF16, name="last_nbr_weights")
         nc.sync.dma_start(last_nbr_weights[:], w_nbr[:, others:])
         nbr_weights = held.tile([P, others], BF16, name="nbr_weights")
-        nc.scalar.dma_start(nbr_weights[:], w_nbr[:, :others])
+        nc.sync.dma_start(nbr_weights[:], w_nbr[:, :others])
         cen_weights = held.tile([P, others], BF16, name="cen_weights")
         nc.sync.dma_start(cen_weights[:], w_cen[:, :others])
         identity = held.tile([P, P], BF16, name="identity")

@@ -22,7 +22,7 @@ def tile_mma_kernel(tc, x, w_cen, w_nbr, offs, out):
     sigmoid = mybir.ActivationFunctionType.Sigmoid
     with (
         tc.tile_pool(name="held", bufs=1) as held,
-        tc.tile_pool(name="work", bufs=6) as work,
+        tc.tile_pool(name="work", bufs=MASKS * DEGREE) as work,
         tc.psum_pool(name="banks", bufs=8) as banks,
     ):
         others = TENSOR_MASKS * P

import concourse.mybir as mybir
from concourse.masks import make_identity

BF16, F32, U16 = mybir.dt.bfloat16, mybir.dt.float32, mybir.dt.uint16

P = 128
NODES = 512
DEGREE = 4
MASKS = 4
LIST = DEGREE * NODES
RUN_COLS = NODES // 16
APART = 24
STEP = 16
HALF = NODES // 2
TENSOR_MASKS = MASKS - 1

FLOPS = 2 * P * (MASKS * P) * (LIST + NODES)


def tile_mma_kernel(tc, x, w_cen, w_nbr, offs, out):
    nc = tc.nc
    sigmoid = mybir.ActivationFunctionType.Sigmoid
    with (
        tc.tile_pool(name="held", bufs=1) as held,
        tc.tile_pool(name="work", bufs=MASKS * DEGREE) as work,
        tc.psum_pool(name="banks", bufs=8) as banks,
    ):
        others = TENSOR_MASKS * P
        nodes = held.tile([P, NODES], BF16, name="nodes")
        for first in range(0, NODES, HALF):
            nc.scalar.dma_start(nodes[:, first : first + HALF], x[:, first : first + HALF])
        last_cen_weights = held.tile([P, P], BF16, name="last_cen_weights")
        nc.sync.dma_start(last_cen_weights[:], w_cen[:, others:])
        offsets = held.tile([P, LIST // 16], U16, name="offsets")
        nc.sync.dma_start(offsets[:], offs)
        last_nbr_weights = held.tile([P, P], BF16, name="last_nbr_weights")
        nc.sync.dma_start(last_nbr_weights[:], w_nbr[:, others:])
        nbr_weights = held.tile([P, others], BF16, name="nbr_weights")
        nc.sync.dma_start(nbr_weights[:], w_nbr[:, :others])
        cen_weights = held.tile([P, others], BF16, name="cen_weights")
        nc.sync.dma_start(cen_weights[:], w_cen[:, :others])
        identity = held.tile([P, P], BF16, name="identity")
        make_identity(nc, identity[:])

        add, mult = mybir.AluOpType.add, mybir.AluOpType.mult

        def centre_part(z, a, pieces, opens, closes):
            edges = [NODES * i // (pieces * STEP) * STEP for i in range(pieces + 1)]
            for first, end in zip(edges[:-1], edges[1:]):
                nc.tensor.matmul(
                    z[:, first:end], cen_weights[:, a * P : (a + 1) * P], nodes[:, first:end],
                    start=(opens and first == 0), stop=(closes and end == NODES),
                )

        def neighbour_part(z, d, weights, first, entries, opens, closes):
            listed = offsets[:, (d * NODES + first) // 16 : (d * NODES + first + entries) // 16]
            nc.tensor.matmul(
                z[:, first : first + entries], weights, nodes[:].indirect(listed),
                start=opens, stop=(closes and first + entries == NODES),
            )

        def nbr_block(a):
            return nbr_weights[:, a * P : (a + 1) * P]

        def finish(z, d, a, parts=1):
            mask = work.tile([P, NODES], F32, name="mask")
            masked = work.tile([P, NODES], F32, name="masked")
            for part in range(parts):
                cols = slice(part * NODES // parts, (part + 1) * NODES // parts)
                nc.scalar.activation(mask[:, cols], z[:, cols], sigmoid)
                nc.vector.tensor_tensor(masked[:, cols], mask[:, cols], neighbours[d][:, cols], mult)
                stored = slice(d * NODES + cols.start, d * NODES + cols.stop)
                nc.sync.dma_start(out[a * P : (a + 1) * P, stored], masked[:, cols])

        def open_by_gather(units):
            sums = [banks.tile([P, NODES], F32, name="bank") for unit in units]
            for z, (d, a) in zip(sums, units):
                neighbour_part(z, d, nbr_block(a), 0, NODES, opens=True, closes=False)
            return sums

        def close_by_centre(sums, units, pieces, parts=1):
            for z, (d, a) in zip(sums, units):
                centre_part(z, a, pieces, opens=False, closes=True)
                finish(z, d, a, parts)

        def open_by_centre(units, pieces):
            sums = [banks.tile([P, NODES], F32, name="bank") for unit in units]
            for z, (d, a) in zip(sums, units):
                centre_part(z, a, pieces, opens=True, closes=False)
            return sums

        def close_by_gather(sums, units):
            for z, (d, a) in zip(sums, units):
                for first in range(0, NODES, HALF):
                    neighbour_part(z, d, nbr_block(a), first, HALF, opens=False, closes=True)
                finish(z, d, a)

        centre_bank = banks.tile([P, NODES], F32, name="bank")
        for first in range(0, NODES, HALF):
            cols = slice(first, first + HALF)
            nc.tensor.matmul(
                centre_bank[:, cols], last_cen_weights[:], nodes[:, cols],
                start=(first == 0), stop=(first + HALF == NODES),
            )
        centre_kept = held.tile([P, NODES], F32, name="centre_kept")
        nc.vector.tensor_copy(centre_kept[:], centre_bank[:])

        last_mask_sums = []
        for d in range(DEGREE):
            product = banks.tile([P, NODES], F32, name="bank")
            neighbour_part(product, d, last_nbr_weights[:], 0, NODES, opens=True, closes=True)
            z = held.tile([P, NODES], F32, name=f"z{d}")
            nc.vector.tensor_tensor(z[:], product[:], centre_kept[:], add)
            last_mask_sums.append(z)

        neighbours = []
        for d in range(DEGREE):
            gathered = banks.tile([P, NODES], F32, name="bank")
            run = offsets[:, d * RUN_COLS : (d + 1) * RUN_COLS]
            nc.tensor.matmul(gathered[:], identity[:], nodes[:].indirect(run), start=True, stop=True)
            kept = held.tile([P, NODES], F32, name=f"neighbours{d}")
            nc.scalar.copy(kept[:], gathered[:])
            neighbours.append(kept)

        for d in range(DEGREE):
            finish(last_mask_sums[d], d, MASKS - 1)

        units = [(d, a) for d in range(DEGREE) for a in range(TENSOR_MASKS)]
        gap_sums = (8, 3)
        first = 0
        for count in gap_sums:
            here = units[first : first + count]
            first += count
            pieces = -(-APART // count)
            before = here[: (count + 1) // 2]
            behind = here[(count + 1) // 2 :]
            sums = open_by_gather(before)
            close_by_centre(sums, before, pieces)
            sums = open_by_centre(behind, pieces)
            close_by_gather(sums, behind)
        tail = units[first:]
        sums = open_by_gather(tail)
        close_by_centre(sums, tail, pieces=2, parts=2)
